import numpy as np
import ml_dtypes


def mxq(x, axis, fmt="e4m3"):
    dtype, down = {"e4m3": (ml_dtypes.float8_e4m3fn, 7), "e5m2": (ml_dtypes.float8_e5m2, 14)}[fmt]
    v = np.moveaxis(np.asarray(x, np.float32).astype(ml_dtypes.bfloat16).astype(np.float64), axis, -1)
    blocks = v.reshape(v.shape[:-1] + (-1, 32))
    amax = np.abs(blocks).max(-1, keepdims=True)
    byte = np.maximum(np.where(amax > 0, np.frexp(amax)[1] - 1 + 127, 0) - down, 1)
    scale = np.exp2(byte - 127.0)
    codes = (blocks / scale).astype(np.float32).astype(dtype).astype(np.float64)
    return np.moveaxis((codes * scale).reshape(v.shape), -1, axis)


WIDE = False


def mx_kscale(k):
    if not WIDE:
        return np.ones(k)
    levels = np.array([18, -18])
    if k % 512:
        return np.exp2(np.random.permutation(np.resize(levels, k // 32))).repeat(32)
    a = np.empty((k // 512, 16))
    for p in range(k // 512):
        a[p, :8] = np.random.permutation(np.resize(levels, 8))
        for g in range(8):
            far = levels[np.abs(levels - a[p, g]) >= 10]
            a[p, g + 8] = far[np.random.randint(len(far))]
    return np.exp2(a.ravel()).repeat(32)


BF16 = ml_dtypes.bfloat16


def bf(x):
    return np.asarray(x, np.float32).astype(BF16)


def f64(x):
    return np.asarray(x).astype(np.float64)


M, N, IN_CH, HID, DEG = 2560, 2560, 512, 512, 24


def setup_inputs():
    u = mx_kscale(M)
    v = mx_kscale(HID)
    s = mx_kscale(N)
    x0 = bf(np.random.standard_normal((N, IN_CH)))
    adj0 = bf(np.random.uniform(size=(M, N)) < DEG / N)
    w0 = bf(np.random.standard_normal((IN_CH, HID)) * 2.0 / np.sqrt(IN_CH))
    b_in = bf(np.random.standard_normal(HID) * 0.3)
    g = bf(np.random.standard_normal((M, HID)) * np.exp2(np.random.randint(-6, 1, (M, 1))) * 4.0 * u[:, None] * v)
    deg = np.sum(f64(adj0), axis=1)
    return {"x": bf(f64(x0) * s[:, None]),
            "adj": bf(f64(adj0) / u[:, None] / s[None, :]),
            "W_in": bf(f64(w0) / v),
            "b_in": b_in,
            "deg": np.asarray(deg, np.float32),
            "grad_out": g}


def reference(x, adj, W_in, b_in, deg, grad_out):
    dz2 = f64(grad_out) / (f64(deg)[:, None] + 1.0)
    dh = mxq(f64(adj), 0, "e4m3").T @ mxq(dz2, 0, "e5m2")
    dz1 = dh
    dx = mxq(dz1, 1, "e5m2") @ mxq(f64(W_in), 1, "e4m3").T
    dW = mxq(f64(x), 0, "e4m3").T @ mxq(dz1, 0, "e5m2")
    return dx, dW

from contextlib import ExitStack

import concourse.mybir as mybir
from concourse.masks import make_identity

N = 2560
IN = 512
HID = 512
FLOPS = 2 * (N * N * HID + 2 * N * IN * HID)
BYTES = 2 * (N * IN + N * N + IN * HID + N * HID) + 4 * (N + N * IN + IN * HID)

F32 = mybir.dt.float32
BF16 = mybir.dt.bfloat16
U32 = mybir.dt.uint32
U8 = mybir.dt.uint8
E4 = mybir.dt.float8_e4m3fn_x4
E5 = mybir.dt.float8_e5m2_x4
MULT = mybir.AluOpType.mult

P = 128
B = 512
NB = N // B


def tile_allgnn_pa_v_kernel(tc, x, adj, W_in, b_in, deg, grad_out, out_0, out_1):
    nc = tc.nc
    with ExitStack() as ctx:
        sb = ctx.enter_context(tc.tile_pool(name="sb", bufs=1))
        ps = ctx.enter_context(tc.psum_pool(name="ps", bufs=1))
        ctx.enter_context(tc.manual_schedule())

        def new(shape, dt, tag, bufs):
            return sb.tile(shape, dt, tag=tag, name=tag, bufs=bufs, align_bytes=64)

        def bank(tag):
            return ps.tile([P, B], F32, tag=tag, name=tag, bufs=1)

        def codes(tag, bufs):
            return new([P, B], U32, tag + "c", bufs), new([P, B], U8, tag + "s", bufs)

        def quantize(src, tag, bufs, fmt):
            c, s = codes(tag, bufs)
            nc.vector.quantize_mx(out=c[:].bitcast(fmt), scales=s[:], in_=src[:])
            return c, s

        def mm(out, l, lcols, lfmt, r, rfmt, start, stop):
            nc.tensor.matmul_mx(
                out=out[:],
                lhsT=l[0][:, lcols].bitcast(lfmt),
                lhsT_scale=l[1][:, lcols],
                rhs=r[0][:].bitcast(rfmt),
                rhs_scale=r[1][:],
                start=start,
                stop=stop,
            )

        def rows(ap, g, cols):
            return ap[B * g : B * (g + 1), cols].rearrange("(p j) w -> p j w", j=4)

        def copy(eng, out, in_):
            if eng == "S":
                nc.scalar.copy(out=out, in_=in_)
            else:
                nc.vector.tensor_copy(out=out, in_=in_)

        def interleave(eng, src):
            dst = new([P, 4 * B], BF16, "ilv", 7)
            copy(
                eng,
                dst[:].rearrange("p (w i j) -> p w j i", i=4, j=4),
                src.rearrange("p j (w i) -> p w j i", i=4),
            )
            return dst

        full = slice(0, B)

        r = new([P, NB, 4], F32, "deg", 1)
        nc.sync.dma_start(out=r[:], in_=deg.rearrange("(g p j) -> p g j", p=P, j=4))
        ident = new([P, P], F32, "ident", 1)
        make_identity(nc, ident[:])

        def load512(ap, g):
            t = new([P, 4, B], BF16, "raw512", 11)
            nc.sync.dma_start(out=t[:], in_=rows(ap, g, full))
            return t

        graw, araw = [], {}
        w_raw = new([P, 4, HID], BF16, "wraw", 1)
        for g in range(NB):
            if g == NB - 1:
                nc.sync.dma_start(out=w_raw[:], in_=W_in.rearrange("(a p) h -> p a h", p=P))
            graw.append(load512(grad_out, g))
            araw[0, g] = load512(adj, g)[:]

        def load_pair(c, g):
            t = new([P, 4, 2 * B], BF16, "raw1024", 8)
            nc.sync.dma_start(out=t[:], in_=rows(adj, g, slice(B * c, B * (c + 2))))
            araw[c, g] = t[:, :, 0:B]
            araw[c + 1, g] = t[:, :, B : 2 * B]

        for g in range(NB):
            load_pair(1, g)

        nc.vector.tensor_scalar_add(r[:], r[:], 1.0)
        rec = new([P, NB, 4], F32, "rec", 1)
        nc.vector.reciprocal(out=rec[:], in_=r[:])

        def scale_g(g):
            t = new([P, 4, HID], BF16, "g2", 2)
            for j in range(4):
                nc.vector.tensor_scalar_mul(t[:, j, :], graw[g][:, j, :], rec[:, g, j : j + 1])
            return t

        def interleave_g(src):
            dst = new([P, 4 * HID], BF16, "ilv", 7)
            nc.vector.tensor_copy(
                out=dst[:].rearrange("p (t m j) -> p t m j", t=4, j=4),
                in_=src[:].rearrange("p j (m t) -> p t m j", t=4),
            )
            return dst

        dh = {}
        gcodes, xcodes, kcodes = [], [], []
        ailv = {}

        def inter(eng, c, g):
            ailv[c, g] = interleave(eng, araw[c, g])

        def quant_mul(c, g):
            a = quantize(ailv[c, g], "a", 4, E4)
            for t in range(4):
                if g == 0:
                    dh[t] = bank("dh" + str(t))
                mm(dh[t], gcodes[g], slice(P * t, P * (t + 1)), E5, a, E4, g == 0, g == NB - 1)

        w_words = w_raw[:].bitcast(F32)
        w_ilv = []
        wc = []

        def w_transpose():
            dst = new([P, 4 * IN], BF16, "ilv", 7)
            dv = dst[:].bitcast(F32).rearrange("p (b a i u) -> p b a i u", b=2, a=2, u=2)
            for b in range(2):
                xt = bank("w" + str(b))[:].rearrange("p (a u i) -> p a u i", a=2, u=2)
                for a in range(2):
                    for u in range(2):
                        nc.tensor.transpose(xt[:, a, u, :], w_words[:, 2 * b + a, u : HID // 2 : 2], ident[:])
                nc.scalar.copy(out=dv[:, b], in_=xt.rearrange("p a u i -> p a i u"))
            w_ilv.append(dst)

        g2 = scale_g(0)
        inter("S", 0, 0)
        gi = interleave_g(g2)
        for g in range(1, NB):
            g2 = scale_g(g)
            inter("S", 0, g)
            gcodes.append(quantize(gi, "g", NB, E5))
            gi = interleave_g(g2)
            quant_mul(0, g - 1)
        x_raw = [load512(x, 0), load512(x, 1)]
        for g in range(3):
            load_pair(3, g)
        for g in range(2, NB):
            x_raw.append(load512(x, g))
        gcodes.append(quantize(gi, "g", NB, E5))
        w_transpose()
        inter("S", 1, 0)
        quant_mul(0, NB - 1)

        def evict(engs):
            d = new([P, 4, B], BF16, "d", 2)
            for t in range(4):
                copy(engs[t], d[:, t, :], dh[t][:])
            return d

        def flip(d, tags):
            words = d[:].bitcast(F32)
            out = []
            for b in range(2):
                xt = bank(tags[b])[:].rearrange("p (t u m) -> p t u m", t=2, u=2)
                for t in range(2):
                    for u in range(2):
                        nc.tensor.transpose(xt[:, t, u, :], words[:, 2 * b + t, u : B // 2 : 2], ident[:])
                out.append(xt)
            return out

        def flip_copy(xts, eng):
            dst = new([P, 4 * HID], BF16, "ilv", 7)
            dv = dst[:].bitcast(F32).rearrange("p (b t m u) -> p b t m u", b=2, t=2, u=2)
            for b in range(2):
                copy(eng, dv[:, b], xts[b].rearrange("p t u m -> p t m u"))
            return dst

        def dx_mul(h, tags):
            out = []
            for b in range(4):
                o = bank(tags[b])
                mm(o, h, slice(P * b, P * (b + 1)), E5, wc[0], E4, True, True)
                out.append(o)
            return out

        def dx_store(c, b, o, eng):
            t = new([P, IN], F32, "out", 6)
            copy(eng, t[:], o[:])
            n0 = B * c + P * b
            nc.sync.dma_start(out=out_0[n0 : n0 + P, :], in_=t[:])

        acc = {}

        def dw_mul(a, cs):
            for c in cs:
                if c == 0:
                    acc[a] = bank("w" + str((a + 2) % 4))
                mm(acc[a], xcodes[c], slice(P * a, P * (a + 1)), E4, kcodes[c], E5, c == 0, c == NB - 1)

        def quant_x(src):
            xcodes.append(quantize(src, "x", NB, E4))

        for c in range(1, NB):
            d = evict("SSSS")
            inter("V", c, 1)
            xts = flip(d, ["w0", "w1"])
            quant_mul(c, 0)
            inter("V", c, 2)
            kn = flip_copy(xts, "S")
            quant_mul(c, 1)
            if c == 2:
                load_pair(3, 3)
            if c == 1:
                wc.append(quantize(w_ilv[0], "wq", 1, E4))
            hi = interleave("V", d[:])
            if c == 2:
                load_pair(3, 4)
            xi = interleave("V", x_raw[c - 1][:])
            inter("S", c, 3)
            h = quantize(hi, "h", 2, E5)
            o = dx_mul(h, ["w2", "w3", "w0", "w1"])
            inter("V", c, 4)
            kcodes.append(quantize(kn, "k", NB, E5))
            quant_mul(c, 2)
            for b in range(4):
                dx_store(c - 1, b, o[b], "S")
            quant_x(xi)
            if c == NB - 1:
                dw_mul(0, range(NB - 1))
                dw_mul(1, range(NB - 1))
            quant_mul(c, 3)
            if c < NB - 1:
                inter("S", c + 1, 0)
            quant_mul(c, 4)

        xi = interleave("V", x_raw[NB - 1][:])
        d = evict("SVSV")
        xts = flip(d, ["dh0", "dh1"])
        dw_mul(2, range(NB - 1))
        dw_mul(3, range(NB - 1))
        hi = interleave("V", d[:])
        kn = flip_copy(xts, "S")
        quant_x(xi)
        h = quantize(hi, "h", 2, E5)
        o = dx_mul(h, ["dh2", "dh3", "dh0", "dh1"])
        kcodes.append(quantize(kn, "k", NB, E5))
        for a in range(4):
            dw_mul(a, [NB - 1])
        for b in range(4):
            dx_store(NB - 1, b, o[b], "SV"[b % 2])
        for a in range(4):
            t = new([P, HID], F32, "out", 6)
            copy(
                "SV"[a % 2],
                t[:].rearrange("p (m t) -> p m t", t=4),
                acc[a][:].rearrange("p (t m) -> p m t", t=4),
            )
            nc.sync.dma_start(out=out_1[P * a : P * (a + 1), :], in_=t[:])
